import numpy as np
import ml_dtypes

BF16 = ml_dtypes.bfloat16


def bf(x):
    return np.asarray(x, np.float32).astype(BF16)


def f32(x):
    return np.asarray(x, np.float32)


def f64(x):
    return np.asarray(x).astype(np.float64)


def striped(idx):
    return np.tile(idx.reshape(-1, 16).T, (8, 1))


S, D, M, N = 512, 128, 128, 64
EPS = 1e-6


def erf(a):
    a = np.asarray(a, np.float64)
    c = np.clip(a, -6.0, 6.0)
    term = c.copy()
    total = c.copy()
    for n in range(1, 150):
        term = term * 2.0 * c * c / (2.0 * n + 1.0)
        total = total + term
    r = 2.0 / np.sqrt(np.pi) * np.exp(-c * c) * total
    return np.where(np.abs(a) > 6.0, np.sign(a), r)


def gelu_erf(v):
    return 0.5 * v * (1.0 + erf(v / np.sqrt(2.0)))


def setup_inputs():
    spread = 0.5 + 1.5 * np.random.random((S, 1))
    centre = 0.5 * np.random.standard_normal((S, 1))
    return {"table": bf(np.random.standard_normal((S, D)) * spread + centre), "gamma": f32(1.0 + 0.1 * np.random.standard_normal((D, 1))), "beta": f32(0.1 * np.random.standard_normal((D, 1))), "lin_w": bf(np.random.standard_normal((D, M)) / np.sqrt(D)), "lin_b": f32(0.1 * np.random.standard_normal((M, 1))), "offs": striped(np.random.permutation(S)[:N])}


def reference(table, gamma, beta, lin_w, lin_b, offs):
    idx = offs[:16].T.reshape(-1)
    t = f64(table)
    mu = t.mean(axis=1, keepdims=True)
    var = ((t - mu) ** 2).mean(axis=1, keepdims=True)
    x = (t - mu) / np.sqrt(var + EPS) * f64(gamma).T + f64(beta).T
    v = f64(lin_w).T @ x[idx].T + f64(lin_b)
    return gelu_erf(v)

@@ -1,0 +1,67 @@
+import concourse.mybir as mybir
+from concourse.masks import make_identity
+
+BF16, F32, U16 = mybir.dt.bfloat16, mybir.dt.float32, mybir.dt.uint16
+ACT = mybir.ActivationFunctionType
+ALU = mybir.AluOpType
+
+P = 128
+TOKENS = 512
+BLOCKS = TOKENS // P
+PICKED = 64
+EPS = 1e-6
+FLOPS = 2 * P * P * PICKED
+
+
+def tile_spaformer_kernel(tc, table, gamma, beta, lin_w, lin_b, offs, out):
+    nc = tc.nc
+    with (
+        tc.tile_pool(name="held", bufs=1) as held,
+        tc.psum_pool(name="psum", bufs=1) as psum,
+    ):
+        rows = held.tile([P, BLOCKS, P], BF16, name="rows")
+        for b in range(BLOCKS):
+            queue = nc.sync if b % 2 == 0 else nc.scalar
+            queue.dma_start(rows[:, b, :], table[b * P : (b + 1) * P, :])
+        offsets = held.tile([P, PICKED // 16], U16, name="offsets")
+        nc.sync.dma_start(offsets[:], offs)
+        weights = held.tile([P, P], BF16, name="weights")
+        nc.scalar.dma_start(weights[:], lin_w)
+        gain = held.tile([P, 1], F32, name="gain")
+        nc.sync.dma_start(gain[:], gamma)
+        shift = held.tile([P, 1], F32, name="shift")
+        nc.scalar.dma_start(shift[:], beta)
+        bias = held.tile([P, 1], F32, name="bias")
+        nc.sync.dma_start(bias[:], lin_b)
+
+        identity = held.tile([P, P], F32, name="identity")
+        make_identity(nc, identity[:])
+        eps = held.tile([P, 1], F32, name="eps")
+        nc.gpsimd.memset(eps[:], EPS)
+
+        partial = held.tile([P, BLOCKS, 6], F32, name="partial")
+        mean_var = held.tile([P, BLOCKS, 2], F32, name="mean_var")
+        for b in range(BLOCKS):
+            nc.vector.bn_stats(partial[:, b, :], rows[:, b, :])
+            nc.vector.bn_aggr(mean_var[:, b, :], partial[:, b, :])
+
+        std = held.tile([P, BLOCKS, 1], F32, name="std")
+        nc.scalar.activation(std[:], mean_var[:, :, 1:2], ACT.Sqrt, bias=eps[:])
+        rstd = held.tile([P, BLOCKS, 1], F32, name="rstd")
+        nc.vector.reciprocal(rstd[:], std[:])
+
+        normed = held.tile([P, BLOCKS, P], F32, name="normed")
+        x = held.tile([P, TOKENS], BF16, name="x")
+        for b in range(BLOCKS):
+            nc.vector.tensor_scalar(
+                normed[:, b, :], rows[:, b, :], mean_var[:, b, 0:1], rstd[:, b, :], ALU.subtract, ALU.mult
+            )
+            flipped = psum.tile([P, P], F32, name=f"flipped{b}")
+            nc.tensor.transpose(flipped[:], normed[:, b, :], identity[:])
+            nc.vector.tensor_scalar(x[:, b * P : (b + 1) * P], flipped[:], gain[:], shift[:], ALU.mult, ALU.add)
+
+        product = psum.tile([P, PICKED], F32, name="product")
+        nc.tensor.matmul(product[:], weights[:], x[:].indirect(offsets[:]), start=True, stop=True)
+        result = held.tile([P, PICKED], F32, name="result")
+        nc.scalar.activation(result[:], product[:], ACT.Gelu, bias=bias[:])
+        nc.sync.dma_start(out, result[:])

@@ -39,6 +39,9 @@ def tile_spaformer_kernel(tc, table, gamma, beta, lin_w, lin_b, offs, out):
         eps = held.tile([P, 1], F32, name="eps")
         nc.gpsimd.memset(eps[:], EPS)
 
+        warm_sqrt = held.tile([P, 1], F32, name="warm_sqrt")
+        nc.scalar.activation(warm_sqrt[:], eps[:], ACT.Sqrt)
+
         partial = held.tile([P, BLOCKS, 6], F32, name="partial")
         mean_var = held.tile([P, BLOCKS, 2], F32, name="mean_var")
         for b in range(BLOCKS):
@@ -47,6 +50,8 @@ def tile_spaformer_kernel(tc, table, gamma, beta, lin_w, lin_b, offs, out):
 
         std = held.tile([P, BLOCKS, 1], F32, name="std")
         nc.scalar.activation(std[:], mean_var[:, :, 1:2], ACT.Sqrt, bias=eps[:])
+        warm_gelu = held.tile([P, 1], F32, name="warm_gelu")
+        nc.scalar.activation(warm_gelu[:], std[:, 0, :], ACT.Gelu)
         rstd = held.tile([P, BLOCKS, 1], F32, name="rstd")
         nc.vector.reciprocal(rstd[:], std[:])
 

@@ -8,6 +8,7 @@ ALU = mybir.AluOpType
 P = 128
 TOKENS = 512
 BLOCKS = TOKENS // P
+HALVES = ((0, 1), (2, 3))
 PICKED = 64
 EPS = 1e-6
 FLOPS = 2 * P * P * PICKED
@@ -20,50 +21,55 @@ def tile_spaformer_kernel(tc, table, gamma, beta, lin_w, lin_b, offs, out):
         tc.psum_pool(name="psum", bufs=1) as psum,
     ):
         rows = held.tile([P, BLOCKS, P], BF16, name="rows")
-        for b in range(BLOCKS):
-            queue = nc.sync if b % 2 == 0 else nc.scalar
-            queue.dma_start(rows[:, b, :], table[b * P : (b + 1) * P, :])
-        offsets = held.tile([P, PICKED // 16], U16, name="offsets")
-        nc.sync.dma_start(offsets[:], offs)
-        weights = held.tile([P, P], BF16, name="weights")
-        nc.scalar.dma_start(weights[:], lin_w)
+        blocked = table.rearrange("(b p) d -> p b d", p=P)
+        for (first, last), queue in zip(HALVES, (nc.sync, nc.scalar)):
+            queue.dma_start(rows[:, first : last + 1, :], blocked[:, first : last + 1, :])
         gain = held.tile([P, 1], F32, name="gain")
         nc.sync.dma_start(gain[:], gamma)
         shift = held.tile([P, 1], F32, name="shift")
         nc.scalar.dma_start(shift[:], beta)
+        offsets = held.tile([P, PICKED // 16], U16, name="offsets")
+        nc.sync.dma_start(offsets[:], offs)
+        weights = held.tile([P, P], BF16, name="weights")
+        nc.scalar.dma_start(weights[:], lin_w)
         bias = held.tile([P, 1], F32, name="bias")
         nc.sync.dma_start(bias[:], lin_b)
 
+        eps = held.tile([P, 1], F32, name="eps")
+        nc.vector.memset(eps[:], EPS)
         identity = held.tile([P, P], F32, name="identity")
         make_identity(nc, identity[:])
-        eps = held.tile([P, 1], F32, name="eps")
-        nc.gpsimd.memset(eps[:], EPS)
 
         warm_sqrt = held.tile([P, 1], F32, name="warm_sqrt")
         nc.scalar.activation(warm_sqrt[:], eps[:], ACT.Sqrt)
 
         partial = held.tile([P, BLOCKS, 6], F32, name="partial")
         mean_var = held.tile([P, BLOCKS, 2], F32, name="mean_var")
-        for b in range(BLOCKS):
-            nc.vector.bn_stats(partial[:, b, :], rows[:, b, :])
-            nc.vector.bn_aggr(mean_var[:, b, :], partial[:, b, :])
-
         std = held.tile([P, BLOCKS, 1], F32, name="std")
-        nc.scalar.activation(std[:], mean_var[:, :, 1:2], ACT.Sqrt, bias=eps[:])
-        warm_gelu = held.tile([P, 1], F32, name="warm_gelu")
-        nc.scalar.activation(warm_gelu[:], std[:, 0, :], ACT.Gelu)
-        rstd = held.tile([P, BLOCKS, 1], F32, name="rstd")
-        nc.vector.reciprocal(rstd[:], std[:])
+        for first, last in HALVES:
+            for b in (first, last):
+                nc.vector.bn_stats(partial[:, b, :], rows[:, b, :])
+            for b in (first, last):
+                nc.vector.bn_aggr(mean_var[:, b, :], partial[:, b, :])
+            nc.scalar.activation(std[:, first : last + 1, :], mean_var[:, first : last + 1, 1:2], ACT.Sqrt, bias=eps[:])
 
+        warm_gelu = held.tile([P, 1], F32, name="warm_gelu")
+        nc.scalar.activation(warm_gelu[:], std[:, BLOCKS - 1, :], ACT.Gelu)
+
+        rstd = held.tile([P, BLOCKS, 1], F32, name="rstd")
         normed = held.tile([P, BLOCKS, P], F32, name="normed")
+        flipped = [psum.tile([P, P], F32, name=f"flipped{b}") for b in range(BLOCKS)]
+        for first, last in HALVES:
+            nc.vector.reciprocal(rstd[:, first : last + 1, :], std[:, first : last + 1, :])
+            for b in (first, last):
+                nc.vector.tensor_scalar(
+                    normed[:, b, :], rows[:, b, :], mean_var[:, b, 0:1], rstd[:, b, :], ALU.subtract, ALU.mult
+                )
+                nc.tensor.transpose(flipped[b][:], normed[:, b, :], identity[:])
+
         x = held.tile([P, TOKENS], BF16, name="x")
         for b in range(BLOCKS):
-            nc.vector.tensor_scalar(
-                normed[:, b, :], rows[:, b, :], mean_var[:, b, 0:1], rstd[:, b, :], ALU.subtract, ALU.mult
-            )
-            flipped = psum.tile([P, P], F32, name=f"flipped{b}")
-            nc.tensor.transpose(flipped[:], normed[:, b, :], identity[:])
-            nc.vector.tensor_scalar(x[:, b * P : (b + 1) * P], flipped[:], gain[:], shift[:], ALU.mult, ALU.add)
+            nc.vector.tensor_scalar(x[:, b * P : (b + 1) * P], flipped[b][:], gain[:], shift[:], ALU.mult, ALU.add)
 
         product = psum.tile([P, PICKED], F32, name="product")
         nc.tensor.matmul(product[:], weights[:], x[:].indirect(offsets[:]), start=True, stop=True)

@@ -11,6 +11,7 @@ BLOCKS = TOKENS // P
 HALVES = ((0, 1), (2, 3))
 PICKED = 64
 EPS = 1e-6
+WARM_MATMULS = 8
 FLOPS = 2 * P * P * PICKED
 
 
@@ -34,6 +35,12 @@ def tile_spaformer_kernel(tc, table, gamma, beta, lin_w, lin_b, offs, out):
         nc.scalar.dma_start(weights[:], lin_w)
         bias = held.tile([P, 1], F32, name="bias")
         nc.sync.dma_start(bias[:], lin_b)
+
+        zeros = held.tile([P, TOKENS], BF16, name="zeros")
+        nc.gpsimd.memset(zeros[:], 0.0)
+        unread = psum.tile([P, TOKENS], F32, name="unread")
+        for _ in range(WARM_MATMULS):
+            nc.tensor.matmul(unread[:], zeros[:, :P], zeros[:], start=True, stop=True)
 
         eps = held.tile([P, 1], F32, name="eps")
         nc.vector.memset(eps[:], EPS)

@@ -11,7 +11,6 @@ BLOCKS = TOKENS // P
 HALVES = ((0, 1), (2, 3))
 PICKED = 64
 EPS = 1e-6
-WARM_MATMULS = 8
 FLOPS = 2 * P * P * PICKED
 
 
@@ -36,12 +35,6 @@ def tile_spaformer_kernel(tc, table, gamma, beta, lin_w, lin_b, offs, out):
         bias = held.tile([P, 1], F32, name="bias")
         nc.sync.dma_start(bias[:], lin_b)
 
-        zeros = held.tile([P, TOKENS], BF16, name="zeros")
-        nc.gpsimd.memset(zeros[:], 0.0)
-        unread = psum.tile([P, TOKENS], F32, name="unread")
-        for _ in range(WARM_MATMULS):
-            nc.tensor.matmul(unread[:], zeros[:, :P], zeros[:], start=True, stop=True)
-
         eps = held.tile([P, 1], F32, name="eps")
         nc.vector.memset(eps[:], EPS)
         identity = held.tile([P, P], F32, name="identity")
@@ -59,9 +52,6 @@ def tile_spaformer_kernel(tc, table, gamma, beta, lin_w, lin_b, offs, out):
             for b in (first, last):
                 nc.vector.bn_aggr(mean_var[:, b, :], partial[:, b, :])
             nc.scalar.activation(std[:, first : last + 1, :], mean_var[:, first : last + 1, 1:2], ACT.Sqrt, bias=eps[:])
-
-        warm_gelu = held.tile([P, 1], F32, name="warm_gelu")
-        nc.scalar.activation(warm_gelu[:], std[:, BLOCKS - 1, :], ACT.Gelu)
 
         rstd = held.tile([P, BLOCKS, 1], F32, name="rstd")
         normed = held.tile([P, BLOCKS, P], F32, name="normed")

@@ -40,29 +40,28 @@ def tile_spaformer_kernel(tc, table, gamma, beta, lin_w, lin_b, offs, out):
         identity = held.tile([P, P], F32, name="identity")
         make_identity(nc, identity[:])
 
-        warm_sqrt = held.tile([P, 1], F32, name="warm_sqrt")
-        nc.scalar.activation(warm_sqrt[:], eps[:], ACT.Sqrt)
+        warm = held.tile([P, 1], F32, name="warm")
+        nc.scalar.activation(warm[:], eps[:], ACT.Abs_reciprocal_sqrt)
 
         partial = held.tile([P, BLOCKS, 6], F32, name="partial")
         mean_var = held.tile([P, BLOCKS, 2], F32, name="mean_var")
-        std = held.tile([P, BLOCKS, 1], F32, name="std")
+        rstd = held.tile([P, BLOCKS, 1], F32, name="rstd")
         for first, last in HALVES:
             for b in (first, last):
                 nc.vector.bn_stats(partial[:, b, :], rows[:, b, :])
             for b in (first, last):
                 nc.vector.bn_aggr(mean_var[:, b, :], partial[:, b, :])
-            nc.scalar.activation(std[:, first : last + 1, :], mean_var[:, first : last + 1, 1:2], ACT.Sqrt, bias=eps[:])
+            nc.scalar.activation(
+                rstd[:, first : last + 1, :], mean_var[:, first : last + 1, 1:2], ACT.Abs_reciprocal_sqrt, bias=eps[:]
+            )
 
-        rstd = held.tile([P, BLOCKS, 1], F32, name="rstd")
         normed = held.tile([P, BLOCKS, P], F32, name="normed")
         flipped = [psum.tile([P, P], F32, name=f"flipped{b}") for b in range(BLOCKS)]
-        for first, last in HALVES:
-            nc.vector.reciprocal(rstd[:, first : last + 1, :], std[:, first : last + 1, :])
-            for b in (first, last):
-                nc.vector.tensor_scalar(
-                    normed[:, b, :], rows[:, b, :], mean_var[:, b, 0:1], rstd[:, b, :], ALU.subtract, ALU.mult
-                )
-                nc.tensor.transpose(flipped[b][:], normed[:, b, :], identity[:])
+        for b in range(BLOCKS):
+            nc.vector.tensor_scalar(
+                normed[:, b, :], rows[:, b, :], mean_var[:, b, 0:1], rstd[:, b, :], ALU.subtract, ALU.mult
+            )
+            nc.tensor.transpose(flipped[b][:], normed[:, b, :], identity[:])
 
         x = held.tile([P, TOKENS], BF16, name="x")
         for b in range(BLOCKS):

@@ -7,11 +7,18 @@ ALU = mybir.AluOpType
 
 P = 128
 TOKENS = 512
-BLOCKS = TOKENS // P
-HALVES = ((0, 1), (2, 3))
+FEATURES = 128
+OUT_FEATURES = 128
 PICKED = 64
+OFFSETS_PER_COLUMN = 16
 EPS = 1e-6
-FLOPS = 2 * P * P * PICKED
+
+BLOCKS = TOKENS // P
+HALVES = ((0, 2), (2, 4))
+BN_STATS_DIM = 6
+BN_AGGR_DIM = 2
+
+FLOPS = 2 * FEATURES * OUT_FEATURES * PICKED
 
 
 def tile_spaformer_kernel(tc, table, gamma, beta, lin_w, lin_b, offs, out):
@@ -20,55 +27,53 @@ def tile_spaformer_kernel(tc, table, gamma, beta, lin_w, lin_b, offs, out):
         tc.tile_pool(name="held", bufs=1) as held,
         tc.psum_pool(name="psum", bufs=1) as psum,
     ):
-        rows = held.tile([P, BLOCKS, P], BF16, name="rows")
+        rows = held.tile([P, BLOCKS, FEATURES], BF16, name="rows")
         blocked = table.rearrange("(b p) d -> p b d", p=P)
-        for (first, last), queue in zip(HALVES, (nc.sync, nc.scalar)):
-            queue.dma_start(rows[:, first : last + 1, :], blocked[:, first : last + 1, :])
-        gain = held.tile([P, 1], F32, name="gain")
+        for (first, end), queue in zip(HALVES, (nc.sync, nc.scalar)):
+            queue.dma_start(rows[:, first:end, :], blocked[:, first:end, :])
+        gain = held.tile([FEATURES, 1], F32, name="gain")
         nc.sync.dma_start(gain[:], gamma)
-        shift = held.tile([P, 1], F32, name="shift")
+        shift = held.tile([FEATURES, 1], F32, name="shift")
         nc.scalar.dma_start(shift[:], beta)
-        offsets = held.tile([P, PICKED // 16], U16, name="offsets")
+        offsets = held.tile([P, PICKED // OFFSETS_PER_COLUMN], U16, name="offsets")
         nc.sync.dma_start(offsets[:], offs)
-        weights = held.tile([P, P], BF16, name="weights")
+        weights = held.tile([FEATURES, OUT_FEATURES], BF16, name="weights")
         nc.scalar.dma_start(weights[:], lin_w)
-        bias = held.tile([P, 1], F32, name="bias")
-        nc.sync.dma_start(bias[:], lin_b)
+        head_bias = held.tile([OUT_FEATURES, 1], F32, name="head_bias")
+        nc.sync.dma_start(head_bias[:], lin_b)
 
         eps = held.tile([P, 1], F32, name="eps")
         nc.vector.memset(eps[:], EPS)
         identity = held.tile([P, P], F32, name="identity")
         make_identity(nc, identity[:])
 
-        warm = held.tile([P, 1], F32, name="warm")
-        nc.scalar.activation(warm[:], eps[:], ACT.Abs_reciprocal_sqrt)
+        unread = held.tile([P, 1], F32, name="unread")
+        nc.scalar.activation(unread[:], eps[:], ACT.Abs_reciprocal_sqrt)
 
-        partial = held.tile([P, BLOCKS, 6], F32, name="partial")
-        mean_var = held.tile([P, BLOCKS, 2], F32, name="mean_var")
+        partial = held.tile([P, BLOCKS, BN_STATS_DIM], F32, name="partial")
+        mean_var = held.tile([P, BLOCKS, BN_AGGR_DIM], F32, name="mean_var")
         rstd = held.tile([P, BLOCKS, 1], F32, name="rstd")
-        for first, last in HALVES:
-            for b in (first, last):
+        for first, end in HALVES:
+            for b in range(first, end):
                 nc.vector.bn_stats(partial[:, b, :], rows[:, b, :])
-            for b in (first, last):
+            for b in range(first, end):
                 nc.vector.bn_aggr(mean_var[:, b, :], partial[:, b, :])
-            nc.scalar.activation(
-                rstd[:, first : last + 1, :], mean_var[:, first : last + 1, 1:2], ACT.Abs_reciprocal_sqrt, bias=eps[:]
-            )
+            nc.scalar.activation(rstd[:, first:end, :], mean_var[:, first:end, 1:2], ACT.Abs_reciprocal_sqrt, bias=eps[:])
 
-        normed = held.tile([P, BLOCKS, P], F32, name="normed")
-        flipped = [psum.tile([P, P], F32, name=f"flipped{b}") for b in range(BLOCKS)]
+        normed = held.tile([P, BLOCKS, FEATURES], F32, name="normed")
+        flipped = [psum.tile([FEATURES, P], F32, name=f"flipped{b}") for b in range(BLOCKS)]
         for b in range(BLOCKS):
             nc.vector.tensor_scalar(
                 normed[:, b, :], rows[:, b, :], mean_var[:, b, 0:1], rstd[:, b, :], ALU.subtract, ALU.mult
             )
             nc.tensor.transpose(flipped[b][:], normed[:, b, :], identity[:])
 
-        x = held.tile([P, TOKENS], BF16, name="x")
+        x = held.tile([FEATURES, TOKENS], BF16, name="x")
         for b in range(BLOCKS):
             nc.vector.tensor_scalar(x[:, b * P : (b + 1) * P], flipped[b][:], gain[:], shift[:], ALU.mult, ALU.add)
 
-        product = psum.tile([P, PICKED], F32, name="product")
+        product = psum.tile([OUT_FEATURES, PICKED], F32, name="product")
         nc.tensor.matmul(product[:], weights[:], x[:].indirect(offsets[:]), start=True, stop=True)
-        result = held.tile([P, PICKED], F32, name="result")
-        nc.scalar.activation(result[:], product[:], ACT.Gelu, bias=bias[:])
+        result = held.tile([OUT_FEATURES, PICKED], F32, name="result")
+        nc.scalar.activation(result[:], product[:], ACT.Gelu, bias=head_bias[:])
         nc.sync.dma_start(out, result[:])

@@ -15,8 +15,8 @@ EPS = 1e-6
 
 BLOCKS = TOKENS // P
 HALVES = ((0, 2), (2, 4))
-BN_STATS_DIM = 6
-BN_AGGR_DIM = 2
+BN_STATS_DIM = 3
+COUNT, MEAN, SQUARES = 0, 1, 2
 
 FLOPS = 2 * FEATURES * OUT_FEATURES * PICKED
 
@@ -50,21 +50,23 @@ def tile_spaformer_kernel(tc, table, gamma, beta, lin_w, lin_b, offs, out):
         unread = held.tile([P, 1], F32, name="unread")
         nc.scalar.activation(unread[:], eps[:], ACT.Abs_reciprocal_sqrt)
 
-        partial = held.tile([P, BLOCKS, BN_STATS_DIM], F32, name="partial")
-        mean_var = held.tile([P, BLOCKS, BN_AGGR_DIM], F32, name="mean_var")
+        stats = held.tile([P, BLOCKS, BN_STATS_DIM], F32, name="stats")
         rstd = held.tile([P, BLOCKS, 1], F32, name="rstd")
         for first, end in HALVES:
-            for b in range(first, end):
-                nc.vector.bn_stats(partial[:, b, :], rows[:, b, :])
-            for b in range(first, end):
-                nc.vector.bn_aggr(mean_var[:, b, :], partial[:, b, :])
-            nc.scalar.activation(rstd[:, first:end, :], mean_var[:, first:end, 1:2], ACT.Abs_reciprocal_sqrt, bias=eps[:])
+            nc.vector.bn_stats(stats[:, first:end, :], rows[:, first:end, :].rearrange("p b d -> p d b"))
+            nc.scalar.activation(
+                rstd[:, first:end, :],
+                stats[:, first:end, SQUARES : SQUARES + 1],
+                ACT.Abs_reciprocal_sqrt,
+                bias=eps[:],
+                scale=1.0 / FEATURES,
+            )
 
         normed = held.tile([P, BLOCKS, FEATURES], F32, name="normed")
         flipped = [psum.tile([FEATURES, P], F32, name=f"flipped{b}") for b in range(BLOCKS)]
         for b in range(BLOCKS):
             nc.vector.tensor_scalar(
-                normed[:, b, :], rows[:, b, :], mean_var[:, b, 0:1], rstd[:, b, :], ALU.subtract, ALU.mult
+                normed[:, b, :], rows[:, b, :], stats[:, b, MEAN : MEAN + 1], rstd[:, b, :], ALU.subtract, ALU.mult
             )
             nc.tensor.transpose(flipped[b][:], normed[:, b, :], identity[:])
 

@@ -29,16 +29,16 @@ def tile_spaformer_kernel(tc, table, gamma, beta, lin_w, lin_b, offs, out):
     ):
         rows = held.tile([P, BLOCKS, FEATURES], BF16, name="rows")
         blocked = table.rearrange("(b p) d -> p b d", p=P)
-        for (first, end), queue in zip(HALVES, (nc.sync, nc.scalar)):
-            queue.dma_start(rows[:, first:end, :], blocked[:, first:end, :])
+        for first, end in HALVES:
+            nc.sync.dma_start(rows[:, first:end, :], blocked[:, first:end, :])
         gain = held.tile([FEATURES, 1], F32, name="gain")
         nc.sync.dma_start(gain[:], gamma)
         shift = held.tile([FEATURES, 1], F32, name="shift")
-        nc.scalar.dma_start(shift[:], beta)
+        nc.sync.dma_start(shift[:], beta)
         offsets = held.tile([P, PICKED // OFFSETS_PER_COLUMN], U16, name="offsets")
         nc.sync.dma_start(offsets[:], offs)
         weights = held.tile([FEATURES, OUT_FEATURES], BF16, name="weights")
-        nc.scalar.dma_start(weights[:], lin_w)
+        nc.sync.dma_start(weights[:], lin_w)
         head_bias = held.tile([OUT_FEATURES, 1], F32, name="head_bias")
         nc.sync.dma_start(head_bias[:], lin_b)
 

@@ -47,9 +47,6 @@ def tile_spaformer_kernel(tc, table, gamma, beta, lin_w, lin_b, offs, out):
         identity = held.tile([P, P], F32, name="identity")
         make_identity(nc, identity[:])
 
-        unread = held.tile([P, 1], F32, name="unread")
-        nc.scalar.activation(unread[:], eps[:], ACT.Abs_reciprocal_sqrt)
-
         stats = held.tile([P, BLOCKS, BN_STATS_DIM], F32, name="stats")
         rstd = held.tile([P, BLOCKS, 1], F32, name="rstd")
         for first, end in HALVES:

import concourse.mybir as mybir
from concourse.masks import make_identity

BF16, F32, U16 = mybir.dt.bfloat16, mybir.dt.float32, mybir.dt.uint16
ACT = mybir.ActivationFunctionType
ALU = mybir.AluOpType

P = 128
TOKENS = 512
FEATURES = 128
OUT_FEATURES = 128
PICKED = 64
OFFSETS_PER_COLUMN = 16
EPS = 1e-6

BLOCKS = TOKENS // P
HALVES = ((0, 2), (2, 4))
BN_STATS_DIM = 3
COUNT, MEAN, SQUARES = 0, 1, 2

FLOPS = 2 * FEATURES * OUT_FEATURES * PICKED


def tile_spaformer_kernel(tc, table, gamma, beta, lin_w, lin_b, offs, out):
    nc = tc.nc
    with (
        tc.tile_pool(name="held", bufs=1) as held,
        tc.psum_pool(name="psum", bufs=1) as psum,
    ):
        rows = held.tile([P, BLOCKS, FEATURES], BF16, name="rows")
        blocked = table.rearrange("(b p) d -> p b d", p=P)
        for first, end in HALVES:
            nc.sync.dma_start(rows[:, first:end, :], blocked[:, first:end, :])
        gain = held.tile([FEATURES, 1], F32, name="gain")
        nc.sync.dma_start(gain[:], gamma)
        shift = held.tile([FEATURES, 1], F32, name="shift")
        nc.sync.dma_start(shift[:], beta)
        offsets = held.tile([P, PICKED // OFFSETS_PER_COLUMN], U16, name="offsets")
        nc.sync.dma_start(offsets[:], offs)
        weights = held.tile([FEATURES, OUT_FEATURES], BF16, name="weights")
        nc.sync.dma_start(weights[:], lin_w)
        head_bias = held.tile([OUT_FEATURES, 1], F32, name="head_bias")
        nc.sync.dma_start(head_bias[:], lin_b)

        eps = held.tile([P, 1], F32, name="eps")
        nc.vector.memset(eps[:], EPS)
        identity = held.tile([P, P], F32, name="identity")
        make_identity(nc, identity[:])

        stats = held.tile([P, BLOCKS, BN_STATS_DIM], F32, name="stats")
        rstd = held.tile([P, BLOCKS, 1], F32, name="rstd")
        for first, end in HALVES:
            nc.vector.bn_stats(stats[:, first:end, :], rows[:, first:end, :].rearrange("p b d -> p d b"))
            nc.scalar.activation(
                rstd[:, first:end, :],
                stats[:, first:end, SQUARES : SQUARES + 1],
                ACT.Abs_reciprocal_sqrt,
                bias=eps[:],
                scale=1.0 / FEATURES,
            )

        normed = held.tile([P, BLOCKS, FEATURES], F32, name="normed")
        flipped = [psum.tile([FEATURES, P], F32, name=f"flipped{b}") for b in range(BLOCKS)]
        for b in range(BLOCKS):
            nc.vector.tensor_scalar(
                normed[:, b, :], rows[:, b, :], stats[:, b, MEAN : MEAN + 1], rstd[:, b, :], ALU.subtract, ALU.mult
            )
            nc.tensor.transpose(flipped[b][:], normed[:, b, :], identity[:])

        x = held.tile([FEATURES, TOKENS], BF16, name="x")
        for b in range(BLOCKS):
            nc.vector.tensor_scalar(x[:, b * P : (b + 1) * P], flipped[b][:], gain[:], shift[:], ALU.mult, ALU.add)

        product = psum.tile([OUT_FEATURES, PICKED], F32, name="product")
        nc.tensor.matmul(product[:], weights[:], x[:].indirect(offsets[:]), start=True, stop=True)
        result = held.tile([OUT_FEATURES, PICKED], F32, name="result")
        nc.scalar.activation(result[:], product[:], ACT.Gelu, bias=head_bias[:])
        nc.sync.dma_start(out, result[:])
